import numpy as np
import ml_dtypes

BF16 = ml_dtypes.bfloat16


def bf(x):
    return np.asarray(x, np.float32).astype(BF16)


def f32(x):
    return np.asarray(x, np.float32)


def f64(x):
    return np.asarray(x).astype(np.float64)


def striped(idx):
    return np.tile(idx.reshape(-1, 16).T, (8, 1))


C, C2, T, S, K, RUN, N = 128, 256, 3, 256, 8, 128, 2048
NS = 0.2
EPS = 1e-6


def setup_inputs():
    idx = np.concatenate([np.random.permutation(S)[:RUN] for _ in range(N // RUN)])
    return {
        "x": f32(np.random.standard_normal((T * C, S))),
        "b1": f32(1.0 + 0.1 * np.random.standard_normal((C, 1))),
        "w1": bf(np.random.standard_normal((C2, C)) / np.sqrt(C2)),
        "u1": bf(np.random.standard_normal((C2, C)) / np.sqrt(C2)),
        "offs": striped(idx),
    }


def reference(x, b1, w1, u1, offs):
    idx = offs[:16].T.reshape(-1)
    xv = f64(x).reshape(T, C, S)
    y = xv * (f64(b1)[None] / np.sqrt((xv * xv).sum(axis=0, keepdims=True) + EPS))
    ctr = np.tile(y, (1, 1, K))
    e = y[:, :, idx] + (-ctr)
    f = np.concatenate([e, ctr], axis=1)
    p = np.einsum('io,tij->toj', f64(w1), f)
    d = np.einsum('io,tij->toj', f64(u1), f)
    dot = (p * d).sum(axis=0, keepdims=True)
    dsq = (d * d).sum(axis=0, keepdims=True)
    a = p - (1.0 - NS) * np.minimum(dot, 0.0) / (dsq + EPS) * d
    return a.reshape(T, C, K, S).mean(axis=2).reshape(T * C, S)

@@ -1,0 +1,162 @@
+import concourse.mybir as mybir
+
+F32 = mybir.dt.float32
+BF16 = mybir.dt.bfloat16
+U16 = mybir.dt.uint16
+ALU = mybir.AluOpType
+ACT = mybir.ActivationFunctionType
+
+C = 128
+T = 3
+S = 256
+K = 8
+N = K * S
+PAIR = 2 * S
+N_PAIRS = K // 2
+EPS = 1e-6
+NEG_SLOPE_PART = 0.8
+
+FLOPS = 2 * 2 * T * (2 * C) * C * N
+
+
+def tile_vn_pctransformer_kernel(tc, x, b1, w1, u1, offs, out):
+    nc = tc.nc
+    with (
+        tc.tile_pool(name="held", bufs=1) as held,
+        tc.tile_pool(name="work", bufs=2) as work,
+        tc.psum_pool(name="psum_p", bufs=T) as psum_p,
+        tc.psum_pool(name="psum_d", bufs=T) as psum_d,
+        tc.psum_pool(name="psum_mean", bufs=1) as psum_mean,
+    ):
+        offsets = held.tile([C, N // 16], U16, name="offsets")
+        nc.sync.dma_start(offsets[:], offs)
+        x_sb = held.tile([C, T, S], F32, name="x_sb")
+        nc.scalar.dma_start(x_sb[:], x.rearrange("(t c) s -> c t s", t=T))
+        b1_sb = held.tile([C, 1], F32, name="b1_sb")
+        nc.sync.dma_start(b1_sb[:], b1)
+        w_sb = held.tile([C, 2, C], BF16, name="w_sb")
+        nc.gpsimd.dma_start(w_sb[:], w1.rearrange("(h i) o -> i h o", h=2))
+        u_sb = held.tile([C, 2, C], BF16, name="u_sb")
+        nc.gpsimd.dma_start(u_sb[:], u1.rearrange("(h i) o -> i h o", h=2))
+
+        eps_sb = held.tile([C, 1], F32, name="eps_sb")
+        nc.vector.memset(eps_sb[:], EPS)
+
+        x_sq = held.tile([C, T, S], F32, name="x_sq")
+        nc.scalar.activation(x_sq[:], x_sb[:], ACT.Square)
+        x_len2 = held.tile([C, S], F32, name="x_len2")
+        nc.vector.tensor_tensor(x_len2[:], x_sq[:, 0, :], x_sq[:, 1, :], ALU.add)
+        nc.vector.tensor_tensor(x_len2[:], x_len2[:], x_sq[:, 2, :], ALU.add)
+        x_rlen = held.tile([C, S], F32, name="x_rlen")
+        nc.scalar.activation(x_rlen[:], x_len2[:], ACT.Abs_reciprocal_sqrt, bias=eps_sb[:])
+
+        y = [held.tile([C, S], F32, name=f"y{t}") for t in range(T)]
+        neg_y = held.tile([C, T, S], F32, name="neg_y")
+        ctr_bf = held.tile([C, T, PAIR], BF16, name="ctr_bf")
+        for t in range(T):
+            nc.vector.scalar_tensor_tensor(
+                y[t][:], x_sb[:, t, :], b1_sb[:, 0:1], x_rlen[:], ALU.mult, ALU.mult
+            )
+            nc.vector.tensor_scalar_mul(neg_y[:, t, :], y[t][:], -1.0)
+            nc.scalar.copy(
+                ctr_bf[:, t, :].rearrange("c (h s) -> c h s", h=2),
+                y[t][:].unsqueeze(1).to_broadcast([C, 2, S]),
+            )
+
+        w_ctr_x8 = held.tile([C, C], BF16, name="w_ctr_x8")
+        nc.vector.tensor_scalar_mul(w_ctr_x8[:], w_sb[:, 1, :], float(K))
+
+        p_sum01 = psum_mean.tile([C, 2, S], F32, name="p_sum01")
+        p_sum2 = psum_mean.tile([C, S], F32, name="p_sum2")
+        nc.tensor.matmul(p_sum01[:], w_ctr_x8[:], ctr_bf[:, 0:2, 0:S], start=True, stop=False)
+        nc.tensor.matmul(p_sum2[:], w_ctr_x8[:], ctr_bf[:, 2, 0:S], start=True, stop=False)
+
+        cd_sum = held.tile([C, T, PAIR], F32, name="cd_sum")
+
+        e_f32 = {}
+        e_bf = {}
+        p_ps = {}
+        d_ps = {}
+        d_sb = {}
+        sums = {}
+
+        def gather(c):
+            e_f32[c] = work.tile([C, T, PAIR], F32, name="e_f32")
+            for t in range(T):
+                for h in range(2):
+                    k = 2 * c + h
+                    nc.vector.tensor_tensor(
+                        e_f32[c][:, t, h * S : (h + 1) * S],
+                        y[t][:].indirect(offsets[:, k * (S // 16) : (k + 1) * (S // 16)]),
+                        neg_y[:, t, :],
+                        ALU.add,
+                    )
+
+        def round_edges(c):
+            e_bf[c] = work.tile([C, T, PAIR], BF16, name="e_bf")
+            for t in range(T):
+                nc.scalar.copy(e_bf[c][:, t, :], e_f32[c][:, t, :])
+
+        def project(c):
+            last = c == N_PAIRS - 1
+            for t in range(T):
+                p_ps[t] = psum_p.tile([C, PAIR], F32, name="p_ps")
+                nc.tensor.matmul(p_ps[t][:], w_sb[:, 0, :], e_bf[c][:, t, :], start=True, stop=False)
+                nc.tensor.matmul(p_ps[t][:], w_sb[:, 1, :], ctr_bf[:, t, :], start=False, stop=True)
+                d_ps[t] = psum_d.tile([C, PAIR], F32, name="d_ps")
+                nc.tensor.matmul(d_ps[t][:], u_sb[:, 0, :], e_bf[c][:, t, :], start=True, stop=False)
+                nc.tensor.matmul(d_ps[t][:], u_sb[:, 1, :], ctr_bf[:, t, :], start=False, stop=True)
+            for h in range(2):
+                cols = slice(h * S, (h + 1) * S)
+                stop = last and h == 1
+                nc.tensor.matmul(p_sum01[:], w_sb[:, 0, :], e_bf[c][:, 0:2, cols], start=False, stop=stop)
+                nc.tensor.matmul(p_sum2[:], w_sb[:, 0, :], e_bf[c][:, 2, cols], start=False, stop=stop)
+
+        def products(c):
+            d_sb[c] = work.tile([C, T, PAIR], F32, name="d_sb")
+            prod = work.tile([C, 2, T, PAIR], F32, name="prod")
+            for t in range(T):
+                nc.scalar.copy(d_sb[c][:, t, :], d_ps[t][:])
+                nc.scalar.activation(prod[:, 1, t, :], d_ps[t][:], ACT.Square)
+                nc.vector.tensor_tensor(prod[:, 0, t, :], p_ps[t][:], d_sb[c][:, t, :], ALU.mult)
+            sums[c] = work.tile([C, 2, PAIR], F32, name="sums")
+            nc.vector.tensor_tensor(sums[c][:], prod[:, :, 0, :], prod[:, :, 1, :], ALU.add)
+            nc.vector.tensor_tensor(sums[c][:], sums[c][:], prod[:, :, 2, :], ALU.add)
+
+        def correction(c):
+            r_len = work.tile([C, PAIR], F32, name="r_len")
+            nc.scalar.activation(r_len[:], sums[c][:, 1, :], ACT.Abs_reciprocal_sqrt, bias=eps_sb[:])
+            r_dsq = work.tile([C, PAIR], F32, name="r_dsq")
+            nc.scalar.activation(r_dsq[:], r_len[:], ACT.Square)
+            coef = work.tile([C, PAIR], F32, name="coef")
+            nc.vector.scalar_tensor_tensor(coef[:], sums[c][:, 0, :], 0.0, r_dsq[:], ALU.min, ALU.mult)
+            coef_t = coef[:].unsqueeze(1).to_broadcast([C, T, PAIR])
+            if c == 0:
+                nc.vector.tensor_tensor(cd_sum[:], d_sb[c][:], coef_t, ALU.mult)
+            else:
+                cd = work.tile([C, T, PAIR], F32, name="cd")
+                nc.vector.tensor_tensor(cd[:], d_sb[c][:], coef_t, ALU.mult)
+                nc.vector.tensor_tensor(cd_sum[:], cd_sum[:], cd[:], ALU.add)
+
+        gather(0)
+        round_edges(0)
+        gather(1)
+        for c in range(N_PAIRS):
+            project(c)
+            if c + 1 < N_PAIRS:
+                round_edges(c + 1)
+            products(c)
+            if c + 2 < N_PAIRS:
+                gather(c + 2)
+            correction(c)
+
+        p_mean = held.tile([C, T, S], F32, name="p_mean")
+        nc.scalar.activation(p_mean[:, 0:2, :], p_sum01[:], ACT.Copy, scale=1.0 / K)
+        nc.scalar.activation(p_mean[:, 2, :], p_sum2[:], ACT.Copy, scale=1.0 / K)
+        cd_all = held.tile([C, T, S], F32, name="cd_all")
+        nc.vector.tensor_tensor(cd_all[:], cd_sum[:, :, 0:S], cd_sum[:, :, S:PAIR], ALU.add)
+        result = held.tile([C, T, S], F32, name="result")
+        nc.vector.scalar_tensor_tensor(
+            result[:], cd_all[:], -NEG_SLOPE_PART / K, p_mean[:], ALU.mult, ALU.add
+        )
+        nc.sync.dma_start(out.rearrange("(t o) s -> o t s", t=T), result[:])

@@ -1,4 +1,5 @@
 import concourse.mybir as mybir
+from concourse.masks import make_identity
 
 F32 = mybir.dt.float32
 BF16 = mybir.dt.bfloat16
@@ -14,7 +15,7 @@ N = K * S
 PAIR = 2 * S
 N_PAIRS = K // 2
 EPS = 1e-6
-NEG_SLOPE_PART = 0.8
+REMOVED = 0.8
 
 FLOPS = 2 * 2 * T * (2 * C) * C * N
 
@@ -26,7 +27,7 @@ def tile_vn_pctransformer_kernel(tc, x, b1, w1, u1, offs, out):
         tc.tile_pool(name="work", bufs=2) as work,
         tc.psum_pool(name="psum_p", bufs=T) as psum_p,
         tc.psum_pool(name="psum_d", bufs=T) as psum_d,
-        tc.psum_pool(name="psum_mean", bufs=1) as psum_mean,
+        tc.psum_pool(name="psum_sum", bufs=1) as psum_sum,
     ):
         offsets = held.tile([C, N // 16], U16, name="offsets")
         nc.sync.dma_start(offsets[:], offs)
@@ -41,6 +42,9 @@ def tile_vn_pctransformer_kernel(tc, x, b1, w1, u1, offs, out):
 
         eps_sb = held.tile([C, 1], F32, name="eps_sb")
         nc.vector.memset(eps_sb[:], EPS)
+        minus_removed = held.tile([C, C], F32, name="minus_removed")
+        make_identity(nc, minus_removed[:])
+        nc.vector.tensor_scalar_mul(minus_removed[:], minus_removed[:], -REMOVED)
 
         x_sq = held.tile([C, T, S], F32, name="x_sq")
         nc.scalar.activation(x_sq[:], x_sb[:], ACT.Square)
@@ -66,19 +70,19 @@ def tile_vn_pctransformer_kernel(tc, x, b1, w1, u1, offs, out):
         w_ctr_x8 = held.tile([C, C], BF16, name="w_ctr_x8")
         nc.vector.tensor_scalar_mul(w_ctr_x8[:], w_sb[:, 1, :], float(K))
 
-        p_sum01 = psum_mean.tile([C, 2, S], F32, name="p_sum01")
-        p_sum2 = psum_mean.tile([C, S], F32, name="p_sum2")
-        nc.tensor.matmul(p_sum01[:], w_ctr_x8[:], ctr_bf[:, 0:2, 0:S], start=True, stop=False)
-        nc.tensor.matmul(p_sum2[:], w_ctr_x8[:], ctr_bf[:, 2, 0:S], start=True, stop=False)
-
-        cd_sum = held.tile([C, T, PAIR], F32, name="cd_sum")
+        a_sum01 = psum_sum.tile([C, 2, S], F32, name="a_sum01")
+        a_sum2 = psum_sum.tile([C, S], F32, name="a_sum2")
+        nc.tensor.matmul(a_sum01[:], w_ctr_x8[:], ctr_bf[:, 0:2, 0:S], start=True, stop=False)
+        nc.tensor.matmul(a_sum2[:], w_ctr_x8[:], ctr_bf[:, 2, 0:S], start=True, stop=False)
 
         e_f32 = {}
         e_bf = {}
         p_ps = {}
         d_ps = {}
         d_sb = {}
+        prod = {}
         sums = {}
+        r_dsq = {}
 
         def gather(c):
             e_f32[c] = work.tile([C, T, PAIR], F32, name="e_f32")
@@ -98,7 +102,6 @@ def tile_vn_pctransformer_kernel(tc, x, b1, w1, u1, offs, out):
                 nc.scalar.copy(e_bf[c][:, t, :], e_f32[c][:, t, :])
 
         def project(c):
-            last = c == N_PAIRS - 1
             for t in range(T):
                 p_ps[t] = psum_p.tile([C, PAIR], F32, name="p_ps")
                 nc.tensor.matmul(p_ps[t][:], w_sb[:, 0, :], e_bf[c][:, t, :], start=True, stop=False)
@@ -108,55 +111,63 @@ def tile_vn_pctransformer_kernel(tc, x, b1, w1, u1, offs, out):
                 nc.tensor.matmul(d_ps[t][:], u_sb[:, 1, :], ctr_bf[:, t, :], start=False, stop=True)
             for h in range(2):
                 cols = slice(h * S, (h + 1) * S)
-                stop = last and h == 1
-                nc.tensor.matmul(p_sum01[:], w_sb[:, 0, :], e_bf[c][:, 0:2, cols], start=False, stop=stop)
-                nc.tensor.matmul(p_sum2[:], w_sb[:, 0, :], e_bf[c][:, 2, cols], start=False, stop=stop)
+                nc.tensor.matmul(a_sum01[:], w_sb[:, 0, :], e_bf[c][:, 0:2, cols], start=False, stop=False)
+                nc.tensor.matmul(a_sum2[:], w_sb[:, 0, :], e_bf[c][:, 2, cols], start=False, stop=False)
 
-        def products(c):
+        def copy_and_square_d(c):
             d_sb[c] = work.tile([C, T, PAIR], F32, name="d_sb")
-            prod = work.tile([C, 2, T, PAIR], F32, name="prod")
+            prod[c] = work.tile([C, 2, T, PAIR], F32, name="prod")
             for t in range(T):
                 nc.scalar.copy(d_sb[c][:, t, :], d_ps[t][:])
-                nc.scalar.activation(prod[:, 1, t, :], d_ps[t][:], ACT.Square)
-                nc.vector.tensor_tensor(prod[:, 0, t, :], p_ps[t][:], d_sb[c][:, t, :], ALU.mult)
-            sums[c] = work.tile([C, 2, PAIR], F32, name="sums")
-            nc.vector.tensor_tensor(sums[c][:], prod[:, :, 0, :], prod[:, :, 1, :], ALU.add)
-            nc.vector.tensor_tensor(sums[c][:], sums[c][:], prod[:, :, 2, :], ALU.add)
+                nc.scalar.activation(prod[c][:, 1, t, :], d_ps[t][:], ACT.Square)
 
-        def correction(c):
+        def dot_and_dsq(c):
+            for t in range(T):
+                nc.vector.tensor_tensor(prod[c][:, 0, t, :], p_ps[t][:], d_sb[c][:, t, :], ALU.mult)
+            sums[c] = work.tile([C, 2, PAIR], F32, name="sums")
+            nc.vector.tensor_tensor(sums[c][:], prod[c][:, :, 0, :], prod[c][:, :, 1, :], ALU.add)
+            nc.vector.tensor_tensor(sums[c][:], sums[c][:], prod[c][:, :, 2, :], ALU.add)
+
+        def invert_dsq(c):
             r_len = work.tile([C, PAIR], F32, name="r_len")
             nc.scalar.activation(r_len[:], sums[c][:, 1, :], ACT.Abs_reciprocal_sqrt, bias=eps_sb[:])
-            r_dsq = work.tile([C, PAIR], F32, name="r_dsq")
-            nc.scalar.activation(r_dsq[:], r_len[:], ACT.Square)
+            r_dsq[c] = work.tile([C, PAIR], F32, name="r_dsq")
+            nc.scalar.activation(r_dsq[c][:], r_len[:], ACT.Square)
+
+        def correct(c):
             coef = work.tile([C, PAIR], F32, name="coef")
-            nc.vector.scalar_tensor_tensor(coef[:], sums[c][:, 0, :], 0.0, r_dsq[:], ALU.min, ALU.mult)
-            coef_t = coef[:].unsqueeze(1).to_broadcast([C, T, PAIR])
-            if c == 0:
-                nc.vector.tensor_tensor(cd_sum[:], d_sb[c][:], coef_t, ALU.mult)
-            else:
-                cd = work.tile([C, T, PAIR], F32, name="cd")
-                nc.vector.tensor_tensor(cd[:], d_sb[c][:], coef_t, ALU.mult)
-                nc.vector.tensor_tensor(cd_sum[:], cd_sum[:], cd[:], ALU.add)
+            nc.vector.scalar_tensor_tensor(coef[:], sums[c][:, 0, :], 0.0, r_dsq[c][:], ALU.min, ALU.mult)
+            cd = work.tile([C, T, PAIR], F32, name="cd")
+            nc.vector.tensor_tensor(
+                cd[:], d_sb[c][:], coef[:].unsqueeze(1).to_broadcast([C, T, PAIR]), ALU.mult
+            )
+            for h in range(2):
+                cols = slice(h * S, (h + 1) * S)
+                stop = c == N_PAIRS - 1 and h == 1
+                nc.tensor.matmul(a_sum01[:], minus_removed[:], cd[:, 0:2, cols], start=False, stop=stop)
+                nc.tensor.matmul(a_sum2[:], minus_removed[:], cd[:, 2, cols], start=False, stop=stop)
 
         gather(0)
         round_edges(0)
+        project(0)
+        copy_and_square_d(0)
         gather(1)
+        round_edges(1)
         for c in range(N_PAIRS):
-            project(c)
+            dot_and_dsq(c)
+            invert_dsq(c)
             if c + 1 < N_PAIRS:
-                round_edges(c + 1)
-            products(c)
+                project(c + 1)
+                copy_and_square_d(c + 1)
             if c + 2 < N_PAIRS:
                 gather(c + 2)
-            correction(c)
+                round_edges(c + 2)
+            correct(c)
 
-        p_mean = held.tile([C, T, S], F32, name="p_mean")
-        nc.scalar.activation(p_mean[:, 0:2, :], p_sum01[:], ACT.Copy, scale=1.0 / K)
-        nc.scalar.activation(p_mean[:, 2, :], p_sum2[:], ACT.Copy, scale=1.0 / K)
-        cd_all = held.tile([C, T, S], F32, name="cd_all")
-        nc.vector.tensor_tensor(cd_all[:], cd_sum[:, :, 0:S], cd_sum[:, :, S:PAIR], ALU.add)
-        result = held.tile([C, T, S], F32, name="result")
-        nc.vector.scalar_tensor_tensor(
-            result[:], cd_all[:], -NEG_SLOPE_PART / K, p_mean[:], ALU.mult, ALU.add
-        )
-        nc.sync.dma_start(out.rearrange("(t o) s -> o t s", t=T), result[:])
+        out_tos = out.rearrange("(t o) s -> o t s", t=T)
+        mean01 = held.tile([C, 2, S], F32, name="mean01")
+        nc.scalar.activation(mean01[:], a_sum01[:], ACT.Copy, scale=1.0 / K)
+        nc.sync.dma_start(out_tos[:, 0:2, :], mean01[:])
+        mean2 = held.tile([C, S], F32, name="mean2")
+        nc.vector.tensor_scalar_mul(mean2[:], a_sum2[:], 1.0 / K)
+        nc.scalar.dma_start(out_tos[:, 2, :], mean2[:])

@@ -25,29 +25,36 @@ def tile_vn_pctransformer_kernel(tc, x, b1, w1, u1, offs, out):
     with (
         tc.tile_pool(name="held", bufs=1) as held,
         tc.tile_pool(name="work", bufs=2) as work,
+        tc.tile_pool(name="lagging", bufs=3) as lagging,
         tc.psum_pool(name="psum_p", bufs=T) as psum_p,
         tc.psum_pool(name="psum_d", bufs=T) as psum_d,
-        tc.psum_pool(name="psum_sum", bufs=1) as psum_sum,
+        tc.psum_pool(name="psum_mean", bufs=1) as psum_mean,
     ):
+        x_tcs = x.rearrange("(t c) s -> t c s", t=T)
+        x_sb = held.tile([C, T, S], F32, name="x_sb")
+        nc.sync.dma_start(x_sb[:, 0, :], x_tcs[0])
+        nc.scalar.dma_start(x_sb[:, 1, :], x_tcs[1])
+        nc.scalar.dma_start(x_sb[:, 2, :], x_tcs[2])
         offsets = held.tile([C, N // 16], U16, name="offsets")
         nc.sync.dma_start(offsets[:], offs)
-        x_sb = held.tile([C, T, S], F32, name="x_sb")
-        nc.scalar.dma_start(x_sb[:], x.rearrange("(t c) s -> c t s", t=T))
         b1_sb = held.tile([C, 1], F32, name="b1_sb")
         nc.sync.dma_start(b1_sb[:], b1)
         w_sb = held.tile([C, 2, C], BF16, name="w_sb")
-        nc.gpsimd.dma_start(w_sb[:], w1.rearrange("(h i) o -> i h o", h=2))
+        nc.sync.dma_start(w_sb[:], w1.rearrange("(h i) o -> i h o", h=2))
         u_sb = held.tile([C, 2, C], BF16, name="u_sb")
-        nc.gpsimd.dma_start(u_sb[:], u1.rearrange("(h i) o -> i h o", h=2))
+        nc.scalar.dma_start(u_sb[:], u1.rearrange("(h i) o -> i h o", h=2))
 
         eps_sb = held.tile([C, 1], F32, name="eps_sb")
-        nc.vector.memset(eps_sb[:], EPS)
+        nc.gpsimd.memset(eps_sb[:], EPS)
         minus_removed = held.tile([C, C], F32, name="minus_removed")
         make_identity(nc, minus_removed[:])
-        nc.vector.tensor_scalar_mul(minus_removed[:], minus_removed[:], -REMOVED)
+        nc.gpsimd.tensor_scalar_mul(minus_removed[:], minus_removed[:], -REMOVED / K)
+        w_edge_mean = held.tile([C, C], BF16, name="w_edge_mean")
+        nc.gpsimd.tensor_scalar_mul(w_edge_mean[:], w_sb[:, 0, :], 1.0 / K)
 
         x_sq = held.tile([C, T, S], F32, name="x_sq")
-        nc.scalar.activation(x_sq[:], x_sb[:], ACT.Square)
+        for t in range(T):
+            nc.vector.tensor_tensor(x_sq[:, t, :], x_sb[:, t, :], x_sb[:, t, :], ALU.mult)
         x_len2 = held.tile([C, S], F32, name="x_len2")
         nc.vector.tensor_tensor(x_len2[:], x_sq[:, 0, :], x_sq[:, 1, :], ALU.add)
         nc.vector.tensor_tensor(x_len2[:], x_len2[:], x_sq[:, 2, :], ALU.add)
@@ -67,13 +74,10 @@ def tile_vn_pctransformer_kernel(tc, x, b1, w1, u1, offs, out):
                 y[t][:].unsqueeze(1).to_broadcast([C, 2, S]),
             )
 
-        w_ctr_x8 = held.tile([C, C], BF16, name="w_ctr_x8")
-        nc.vector.tensor_scalar_mul(w_ctr_x8[:], w_sb[:, 1, :], float(K))
-
-        a_sum01 = psum_sum.tile([C, 2, S], F32, name="a_sum01")
-        a_sum2 = psum_sum.tile([C, S], F32, name="a_sum2")
-        nc.tensor.matmul(a_sum01[:], w_ctr_x8[:], ctr_bf[:, 0:2, 0:S], start=True, stop=False)
-        nc.tensor.matmul(a_sum2[:], w_ctr_x8[:], ctr_bf[:, 2, 0:S], start=True, stop=False)
+        a_mean01 = psum_mean.tile([C, 2, S], F32, name="a_mean01")
+        a_mean2 = psum_mean.tile([C, S], F32, name="a_mean2")
+        nc.tensor.matmul(a_mean01[:], w_sb[:, 1, :], ctr_bf[:, 0:2, 0:S], start=True, stop=False)
+        nc.tensor.matmul(a_mean2[:], w_sb[:, 1, :], ctr_bf[:, 2, 0:S], start=True, stop=False)
 
         e_f32 = {}
         e_bf = {}
@@ -83,6 +87,7 @@ def tile_vn_pctransformer_kernel(tc, x, b1, w1, u1, offs, out):
         prod = {}
         sums = {}
         r_dsq = {}
+        cd = {}
 
         def gather(c):
             e_f32[c] = work.tile([C, T, PAIR], F32, name="e_f32")
@@ -111,11 +116,11 @@ def tile_vn_pctransformer_kernel(tc, x, b1, w1, u1, offs, out):
                 nc.tensor.matmul(d_ps[t][:], u_sb[:, 1, :], ctr_bf[:, t, :], start=False, stop=True)
             for h in range(2):
                 cols = slice(h * S, (h + 1) * S)
-                nc.tensor.matmul(a_sum01[:], w_sb[:, 0, :], e_bf[c][:, 0:2, cols], start=False, stop=False)
-                nc.tensor.matmul(a_sum2[:], w_sb[:, 0, :], e_bf[c][:, 2, cols], start=False, stop=False)
+                nc.tensor.matmul(a_mean01[:], w_edge_mean[:], e_bf[c][:, 0:2, cols], start=False, stop=False)
+                nc.tensor.matmul(a_mean2[:], w_edge_mean[:], e_bf[c][:, 2, cols], start=False, stop=False)
 
         def copy_and_square_d(c):
-            d_sb[c] = work.tile([C, T, PAIR], F32, name="d_sb")
+            d_sb[c] = lagging.tile([C, T, PAIR], F32, name="d_sb")
             prod[c] = work.tile([C, 2, T, PAIR], F32, name="prod")
             for t in range(T):
                 nc.scalar.copy(d_sb[c][:, t, :], d_ps[t][:])
@@ -124,50 +129,60 @@ def tile_vn_pctransformer_kernel(tc, x, b1, w1, u1, offs, out):
         def dot_and_dsq(c):
             for t in range(T):
                 nc.vector.tensor_tensor(prod[c][:, 0, t, :], p_ps[t][:], d_sb[c][:, t, :], ALU.mult)
-            sums[c] = work.tile([C, 2, PAIR], F32, name="sums")
+            sums[c] = lagging.tile([C, 2, PAIR], F32, name="sums")
             nc.vector.tensor_tensor(sums[c][:], prod[c][:, :, 0, :], prod[c][:, :, 1, :], ALU.add)
             nc.vector.tensor_tensor(sums[c][:], sums[c][:], prod[c][:, :, 2, :], ALU.add)
 
         def invert_dsq(c):
             r_len = work.tile([C, PAIR], F32, name="r_len")
             nc.scalar.activation(r_len[:], sums[c][:, 1, :], ACT.Abs_reciprocal_sqrt, bias=eps_sb[:])
-            r_dsq[c] = work.tile([C, PAIR], F32, name="r_dsq")
+            r_dsq[c] = lagging.tile([C, PAIR], F32, name="r_dsq")
             nc.scalar.activation(r_dsq[c][:], r_len[:], ACT.Square)
 
-        def correct(c):
+        def part_along_d(c):
             coef = work.tile([C, PAIR], F32, name="coef")
             nc.vector.scalar_tensor_tensor(coef[:], sums[c][:, 0, :], 0.0, r_dsq[c][:], ALU.min, ALU.mult)
-            cd = work.tile([C, T, PAIR], F32, name="cd")
+            cd[c] = work.tile([C, T, PAIR], F32, name="cd")
             nc.vector.tensor_tensor(
-                cd[:], d_sb[c][:], coef[:].unsqueeze(1).to_broadcast([C, T, PAIR]), ALU.mult
+                cd[c][:], d_sb[c][:], coef[:].unsqueeze(1).to_broadcast([C, T, PAIR]), ALU.mult
             )
+
+        def remove_on_tensor(c, stop):
             for h in range(2):
                 cols = slice(h * S, (h + 1) * S)
-                stop = c == N_PAIRS - 1 and h == 1
-                nc.tensor.matmul(a_sum01[:], minus_removed[:], cd[:, 0:2, cols], start=False, stop=stop)
-                nc.tensor.matmul(a_sum2[:], minus_removed[:], cd[:, 2, cols], start=False, stop=stop)
+                last = stop and h == 1
+                nc.tensor.matmul(a_mean01[:], minus_removed[:], cd[c][:, 0:2, cols], start=False, stop=last)
+                nc.tensor.matmul(a_mean2[:], minus_removed[:], cd[c][:, 2, cols], start=False, stop=last)
 
         gather(0)
         round_edges(0)
         project(0)
         copy_and_square_d(0)
-        gather(1)
-        round_edges(1)
         for c in range(N_PAIRS):
+            if c + 1 < N_PAIRS:
+                gather(c + 1)
+                round_edges(c + 1)
             dot_and_dsq(c)
             invert_dsq(c)
             if c + 1 < N_PAIRS:
                 project(c + 1)
                 copy_and_square_d(c + 1)
-            if c + 2 < N_PAIRS:
-                gather(c + 2)
-                round_edges(c + 2)
-            correct(c)
+            if c >= 1:
+                part_along_d(c - 1)
+                remove_on_tensor(c - 1, stop=c == N_PAIRS - 1)
 
-        out_tos = out.rearrange("(t o) s -> o t s", t=T)
-        mean01 = held.tile([C, 2, S], F32, name="mean01")
-        nc.scalar.activation(mean01[:], a_sum01[:], ACT.Copy, scale=1.0 / K)
-        nc.sync.dma_start(out_tos[:, 0:2, :], mean01[:])
-        mean2 = held.tile([C, S], F32, name="mean2")
-        nc.vector.tensor_scalar_mul(mean2[:], a_sum2[:], 1.0 / K)
-        nc.scalar.dma_start(out_tos[:, 2, :], mean2[:])
+        final = N_PAIRS - 1
+        part_along_d(final)
+        cd_both = held.tile([C, T, S], F32, name="cd_both")
+        nc.vector.tensor_tensor(cd_both[:], cd[final][:, :, 0:S], cd[final][:, :, S:PAIR], ALU.add)
+        out_ots = out.rearrange("(t o) s -> o t s", t=T)
+        result01 = held.tile([C, 2, S], F32, name="result01")
+        nc.vector.scalar_tensor_tensor(
+            result01[:], cd_both[:, 0:2, :], -REMOVED / K, a_mean01[:], ALU.mult, ALU.add
+        )
+        nc.sync.dma_start(out_ots[:, 0:2, :], result01[:])
+        result2 = held.tile([C, S], F32, name="result2")
+        nc.vector.scalar_tensor_tensor(
+            result2[:], cd_both[:, 2, :], -REMOVED / K, a_mean2[:], ALU.mult, ALU.add
+        )
+        nc.scalar.dma_start(out_ots[:, 2, :], result2[:])

@@ -34,18 +34,20 @@ def tile_vn_pctransformer_kernel(tc, x, b1, w1, u1, offs, out):
         x_sb = held.tile([C, T, S], F32, name="x_sb")
         nc.sync.dma_start(x_sb[:, 0, :], x_tcs[0])
         nc.scalar.dma_start(x_sb[:, 1, :], x_tcs[1])
-        nc.scalar.dma_start(x_sb[:, 2, :], x_tcs[2])
+        nc.sync.dma_start(x_sb[:, 2, :], x_tcs[2])
+        b1_sb = held.tile([C, 1], F32, name="b1_sb")
+        nc.scalar.dma_start(b1_sb[:], b1)
         offsets = held.tile([C, N // 16], U16, name="offsets")
         nc.sync.dma_start(offsets[:], offs)
-        b1_sb = held.tile([C, 1], F32, name="b1_sb")
-        nc.sync.dma_start(b1_sb[:], b1)
         w_sb = held.tile([C, 2, C], BF16, name="w_sb")
         nc.sync.dma_start(w_sb[:], w1.rearrange("(h i) o -> i h o", h=2))
         u_sb = held.tile([C, 2, C], BF16, name="u_sb")
-        nc.scalar.dma_start(u_sb[:], u1.rearrange("(h i) o -> i h o", h=2))
+        nc.sync.dma_start(u_sb[:], u1.rearrange("(h i) o -> i h o", h=2))
 
         eps_sb = held.tile([C, 1], F32, name="eps_sb")
         nc.gpsimd.memset(eps_sb[:], EPS)
+        table_warmer = held.tile([C, 1], F32, name="table_warmer")
+        nc.scalar.activation(table_warmer[:], eps_sb[:], ACT.Abs_reciprocal_sqrt)
         minus_removed = held.tile([C, C], F32, name="minus_removed")
         make_identity(nc, minus_removed[:])
         nc.gpsimd.tensor_scalar_mul(minus_removed[:], minus_removed[:], -REMOVED / K)
@@ -150,18 +152,25 @@ def tile_vn_pctransformer_kernel(tc, x, b1, w1, u1, offs, out):
         def remove_on_tensor(c, stop):
             for h in range(2):
                 cols = slice(h * S, (h + 1) * S)
-                last = stop and h == 1
-                nc.tensor.matmul(a_mean01[:], minus_removed[:], cd[c][:, 0:2, cols], start=False, stop=last)
-                nc.tensor.matmul(a_mean2[:], minus_removed[:], cd[c][:, 2, cols], start=False, stop=last)
+                nc.tensor.matmul(
+                    a_mean01[:], minus_removed[:], cd[c][:, 0:2, cols], start=False, stop=stop and h == 1
+                )
+            for h in range(2):
+                cols = slice(h * S, (h + 1) * S)
+                nc.tensor.matmul(
+                    a_mean2[:], minus_removed[:], cd[c][:, 2, cols], start=False, stop=stop and h == 1
+                )
 
         gather(0)
         round_edges(0)
         project(0)
         copy_and_square_d(0)
+        gather(1)
+        round_edges(1)
         for c in range(N_PAIRS):
-            if c + 1 < N_PAIRS:
-                gather(c + 1)
-                round_edges(c + 1)
+            if c + 2 < N_PAIRS:
+                gather(c + 2)
+                round_edges(c + 2)
             dot_and_dsq(c)
             invert_dsq(c)
             if c + 1 < N_PAIRS:

@@ -14,6 +14,7 @@ K = 8
 N = K * S
 PAIR = 2 * S
 N_PAIRS = K // 2
+TENSOR_SUMS = 1
 EPS = 1e-6
 REMOVED = 0.8
 
@@ -24,7 +25,7 @@ def tile_vn_pctransformer_kernel(tc, x, b1, w1, u1, offs, out):
     nc = tc.nc
     with (
         tc.tile_pool(name="held", bufs=1) as held,
-        tc.tile_pool(name="work", bufs=2) as work,
+        tc.tile_pool(name="work", bufs=3) as work,
         tc.tile_pool(name="lagging", bufs=3) as lagging,
         tc.psum_pool(name="psum_p", bufs=T) as psum_p,
         tc.psum_pool(name="psum_d", bufs=T) as psum_d,
@@ -48,9 +49,10 @@ def tile_vn_pctransformer_kernel(tc, x, b1, w1, u1, offs, out):
         nc.gpsimd.memset(eps_sb[:], EPS)
         table_warmer = held.tile([C, 1], F32, name="table_warmer")
         nc.scalar.activation(table_warmer[:], eps_sb[:], ACT.Abs_reciprocal_sqrt)
+        identity = held.tile([C, C], F32, name="identity")
+        make_identity(nc, identity[:])
         minus_removed = held.tile([C, C], F32, name="minus_removed")
-        make_identity(nc, minus_removed[:])
-        nc.gpsimd.tensor_scalar_mul(minus_removed[:], minus_removed[:], -REMOVED / K)
+        nc.gpsimd.tensor_scalar_mul(minus_removed[:], identity[:], -REMOVED / K)
         w_edge_mean = held.tile([C, C], BF16, name="w_edge_mean")
         nc.gpsimd.tensor_scalar_mul(w_edge_mean[:], w_sb[:, 0, :], 1.0 / K)
 
@@ -87,6 +89,7 @@ def tile_vn_pctransformer_kernel(tc, x, b1, w1, u1, offs, out):
         d_ps = {}
         d_sb = {}
         prod = {}
+        dsq = {}
         sums = {}
         r_dsq = {}
         cd = {}
@@ -128,16 +131,25 @@ def tile_vn_pctransformer_kernel(tc, x, b1, w1, u1, offs, out):
                 nc.scalar.copy(d_sb[c][:, t, :], d_ps[t][:])
                 nc.scalar.activation(prod[c][:, 1, t, :], d_ps[t][:], ACT.Square)
 
+        def dsq_on_tensor(c):
+            dsq_ps = psum_d.tile([C, PAIR], F32, name="dsq_ps", tag="d_ps")
+            dsq[c] = dsq_ps[:]
+            for t in range(T):
+                nc.tensor.matmul(dsq[c], identity[:], prod[c][:, 1, t, :], start=t == 0, stop=t == T - 1)
+
         def dot_and_dsq(c):
             for t in range(T):
                 nc.vector.tensor_tensor(prod[c][:, 0, t, :], p_ps[t][:], d_sb[c][:, t, :], ALU.mult)
             sums[c] = lagging.tile([C, 2, PAIR], F32, name="sums")
-            nc.vector.tensor_tensor(sums[c][:], prod[c][:, :, 0, :], prod[c][:, :, 1, :], ALU.add)
-            nc.vector.tensor_tensor(sums[c][:], sums[c][:], prod[c][:, :, 2, :], ALU.add)
+            n_sums = 1 if c < TENSOR_SUMS else 2
+            nc.vector.tensor_tensor(sums[c][:, 0:n_sums, :], prod[c][:, 0:n_sums, 0, :], prod[c][:, 0:n_sums, 1, :], ALU.add)
+            nc.vector.tensor_tensor(sums[c][:, 0:n_sums, :], sums[c][:, 0:n_sums, :], prod[c][:, 0:n_sums, 2, :], ALU.add)
+            if c >= TENSOR_SUMS:
+                dsq[c] = sums[c][:, 1, :]
 
         def invert_dsq(c):
             r_len = work.tile([C, PAIR], F32, name="r_len")
-            nc.scalar.activation(r_len[:], sums[c][:, 1, :], ACT.Abs_reciprocal_sqrt, bias=eps_sb[:])
+            nc.scalar.activation(r_len[:], dsq[c], ACT.Abs_reciprocal_sqrt, bias=eps_sb[:])
             r_dsq[c] = lagging.tile([C, PAIR], F32, name="r_dsq")
             nc.scalar.activation(r_dsq[c][:], r_len[:], ACT.Square)
 
@@ -165,6 +177,7 @@ def tile_vn_pctransformer_kernel(tc, x, b1, w1, u1, offs, out):
         round_edges(0)
         project(0)
         copy_and_square_d(0)
+        dsq_on_tensor(0)
         gather(1)
         round_edges(1)
         for c in range(N_PAIRS):
@@ -176,9 +189,11 @@ def tile_vn_pctransformer_kernel(tc, x, b1, w1, u1, offs, out):
             if c + 1 < N_PAIRS:
                 project(c + 1)
                 copy_and_square_d(c + 1)
+            if c >= 2:
+                remove_on_tensor(c - 2, stop=False)
             if c >= 1:
                 part_along_d(c - 1)
-                remove_on_tensor(c - 1, stop=c == N_PAIRS - 1)
+        remove_on_tensor(N_PAIRS - 2, stop=True)
 
         final = N_PAIRS - 1
         part_along_d(final)

@@ -72,7 +72,10 @@ def tile_vn_pctransformer_kernel(tc, x, b1, w1, u1, offs, out):
             nc.vector.scalar_tensor_tensor(
                 y[t][:], x_sb[:, t, :], b1_sb[:, 0:1], x_rlen[:], ALU.mult, ALU.mult
             )
-            nc.vector.tensor_scalar_mul(neg_y[:, t, :], y[t][:], -1.0)
+            if t == 0:
+                nc.vector.tensor_scalar_mul(neg_y[:, t, :], y[t][:], -1.0)
+            else:
+                nc.scalar.mul(neg_y[:, t, :], y[t][:], -1.0)
             nc.scalar.copy(
                 ctr_bf[:, t, :].rearrange("c (h s) -> c h s", h=2),
                 y[t][:].unsqueeze(1).to_broadcast([C, 2, S]),

@@ -72,10 +72,7 @@ def tile_vn_pctransformer_kernel(tc, x, b1, w1, u1, offs, out):
             nc.vector.scalar_tensor_tensor(
                 y[t][:], x_sb[:, t, :], b1_sb[:, 0:1], x_rlen[:], ALU.mult, ALU.mult
             )
-            if t == 0:
-                nc.vector.tensor_scalar_mul(neg_y[:, t, :], y[t][:], -1.0)
-            else:
-                nc.scalar.mul(neg_y[:, t, :], y[t][:], -1.0)
+            nc.scalar.mul(neg_y[:, t, :], y[t][:], -1.0)
             nc.scalar.copy(
                 ctr_bf[:, t, :].rearrange("c (h s) -> c h s", h=2),
                 y[t][:].unsqueeze(1).to_broadcast([C, 2, S]),

@@ -25,7 +25,7 @@ def tile_vn_pctransformer_kernel(tc, x, b1, w1, u1, offs, out):
     nc = tc.nc
     with (
         tc.tile_pool(name="held", bufs=1) as held,
-        tc.tile_pool(name="work", bufs=3) as work,
+        tc.tile_pool(name="work", bufs=N_PAIRS) as work,
         tc.tile_pool(name="lagging", bufs=3) as lagging,
         tc.psum_pool(name="psum_p", bufs=T) as psum_p,
         tc.psum_pool(name="psum_d", bufs=T) as psum_d,

@@ -14,7 +14,7 @@ K = 8
 N = K * S
 PAIR = 2 * S
 N_PAIRS = K // 2
-TENSOR_SUMS = 1
+TENSOR_SUMS = 2
 EPS = 1e-6
 REMOVED = 0.8
 
@@ -189,6 +189,8 @@ def tile_vn_pctransformer_kernel(tc, x, b1, w1, u1, offs, out):
             if c + 1 < N_PAIRS:
                 project(c + 1)
                 copy_and_square_d(c + 1)
+                if c + 1 < TENSOR_SUMS:
+                    dsq_on_tensor(c + 1)
             if c >= 2:
                 remove_on_tensor(c - 2, stop=False)
             if c >= 1:

@@ -14,7 +14,7 @@ K = 8
 N = K * S
 PAIR = 2 * S
 N_PAIRS = K // 2
-TENSOR_SUMS = 2
+TENSOR_SUMS = 1
 EPS = 1e-6
 REMOVED = 0.8
 
@@ -26,7 +26,7 @@ def tile_vn_pctransformer_kernel(tc, x, b1, w1, u1, offs, out):
     with (
         tc.tile_pool(name="held", bufs=1) as held,
         tc.tile_pool(name="work", bufs=N_PAIRS) as work,
-        tc.tile_pool(name="lagging", bufs=3) as lagging,
+        tc.tile_pool(name="lagging", bufs=N_PAIRS) as lagging,
         tc.psum_pool(name="psum_p", bufs=T) as psum_p,
         tc.psum_pool(name="psum_d", bufs=T) as psum_d,
         tc.psum_pool(name="psum_mean", bufs=1) as psum_mean,
@@ -88,9 +88,11 @@ def tile_vn_pctransformer_kernel(tc, x, b1, w1, u1, offs, out):
         p_ps = {}
         d_ps = {}
         d_sb = {}
-        prod = {}
+        p_d = {}
+        d_d = {}
+        dot = {}
+        coef = {}
         dsq = {}
-        sums = {}
         r_dsq = {}
         cd = {}
 
@@ -126,26 +128,27 @@ def tile_vn_pctransformer_kernel(tc, x, b1, w1, u1, offs, out):
 
         def copy_and_square_d(c):
             d_sb[c] = lagging.tile([C, T, PAIR], F32, name="d_sb")
-            prod[c] = work.tile([C, 2, T, PAIR], F32, name="prod")
+            d_d[c] = work.tile([C, T, PAIR], F32, name="d_d")
             for t in range(T):
                 nc.scalar.copy(d_sb[c][:, t, :], d_ps[t][:])
-                nc.scalar.activation(prod[c][:, 1, t, :], d_ps[t][:], ACT.Square)
+                nc.scalar.activation(d_d[c][:, t, :], d_ps[t][:], ACT.Square)
 
         def dsq_on_tensor(c):
             dsq_ps = psum_d.tile([C, PAIR], F32, name="dsq_ps", tag="d_ps")
             dsq[c] = dsq_ps[:]
             for t in range(T):
-                nc.tensor.matmul(dsq[c], identity[:], prod[c][:, 1, t, :], start=t == 0, stop=t == T - 1)
+                nc.tensor.matmul(dsq[c], identity[:], d_d[c][:, t, :], start=t == 0, stop=t == T - 1)
 
-        def dot_and_dsq(c):
+        def add_first_two(total, terms):
+            nc.vector.tensor_tensor(total[:], terms[:, 0, :], terms[:, 1, :], ALU.add)
+
+        def add_third(total, terms):
+            nc.vector.tensor_tensor(total[:], total[:], terms[:, 2, :], ALU.add)
+
+        def products(c):
+            p_d[c] = work.tile([C, T, PAIR], F32, name="p_d")
             for t in range(T):
-                nc.vector.tensor_tensor(prod[c][:, 0, t, :], p_ps[t][:], d_sb[c][:, t, :], ALU.mult)
-            sums[c] = lagging.tile([C, 2, PAIR], F32, name="sums")
-            n_sums = 1 if c < TENSOR_SUMS else 2
-            nc.vector.tensor_tensor(sums[c][:, 0:n_sums, :], prod[c][:, 0:n_sums, 0, :], prod[c][:, 0:n_sums, 1, :], ALU.add)
-            nc.vector.tensor_tensor(sums[c][:, 0:n_sums, :], sums[c][:, 0:n_sums, :], prod[c][:, 0:n_sums, 2, :], ALU.add)
-            if c >= TENSOR_SUMS:
-                dsq[c] = sums[c][:, 1, :]
+                nc.vector.tensor_tensor(p_d[c][:, t, :], p_ps[t][:], d_sb[c][:, t, :], ALU.mult)
 
         def invert_dsq(c):
             r_len = work.tile([C, PAIR], F32, name="r_len")
@@ -153,13 +156,14 @@ def tile_vn_pctransformer_kernel(tc, x, b1, w1, u1, offs, out):
             r_dsq[c] = lagging.tile([C, PAIR], F32, name="r_dsq")
             nc.scalar.activation(r_dsq[c][:], r_len[:], ACT.Square)
 
-        def part_along_d(c):
-            coef = work.tile([C, PAIR], F32, name="coef")
-            nc.vector.scalar_tensor_tensor(coef[:], sums[c][:, 0, :], 0.0, r_dsq[c][:], ALU.min, ALU.mult)
-            cd[c] = work.tile([C, T, PAIR], F32, name="cd")
-            nc.vector.tensor_tensor(
-                cd[c][:], d_sb[c][:], coef[:].unsqueeze(1).to_broadcast([C, T, PAIR]), ALU.mult
-            )
+        def coefficient(c):
+            coef[c] = work.tile([C, PAIR], F32, name="coef")
+            nc.vector.scalar_tensor_tensor(coef[c][:], dot[c][:], 0.0, r_dsq[c][:], ALU.min, ALU.mult)
+
+        def part_along_d(c, t):
+            if t == 0:
+                cd[c] = work.tile([C, T, PAIR], F32, name="cd")
+            nc.vector.tensor_tensor(cd[c][:, t, :], d_sb[c][:, t, :], coef[c][:], ALU.mult)
 
         def remove_on_tensor(c, stop):
             for h in range(2):
@@ -173,42 +177,70 @@ def tile_vn_pctransformer_kernel(tc, x, b1, w1, u1, offs, out):
                     a_mean2[:], minus_removed[:], cd[c][:, 2, cols], start=False, stop=stop and h == 1
                 )
 
+        def project_and_square(c):
+            project(c)
+            copy_and_square_d(c)
+            if c < TENSOR_SUMS:
+                dsq_on_tensor(c)
+
         gather(0)
         round_edges(0)
-        project(0)
-        copy_and_square_d(0)
-        dsq_on_tensor(0)
+        project_and_square(0)
+        invert_dsq(0)
         gather(1)
         round_edges(1)
         for c in range(N_PAIRS):
             if c + 2 < N_PAIRS:
                 gather(c + 2)
                 round_edges(c + 2)
-            dot_and_dsq(c)
-            invert_dsq(c)
-            if c + 1 < N_PAIRS:
-                project(c + 1)
-                copy_and_square_d(c + 1)
-                if c + 1 < TENSOR_SUMS:
-                    dsq_on_tensor(c + 1)
-            if c >= 2:
-                remove_on_tensor(c - 2, stop=False)
+            products(c)
+            dot[c] = lagging.tile([C, PAIR], F32, name="dot")
+            add_first_two(dot[c], p_d[c])
             if c >= 1:
-                part_along_d(c - 1)
-        remove_on_tensor(N_PAIRS - 2, stop=True)
+                part_along_d(c - 1, 0)
+            add_third(dot[c], p_d[c])
+            if c >= 1:
+                part_along_d(c - 1, 1)
+                part_along_d(c - 1, 2)
+            coefficient(c)
+            if c + 1 < N_PAIRS:
+                project_and_square(c + 1)
+            if c >= 1:
+                remove_on_tensor(c - 1, stop=c == N_PAIRS - 1)
+            if c + 1 < N_PAIRS:
+                if c + 1 >= TENSOR_SUMS:
+                    dsq_sb = lagging.tile([C, PAIR], F32, name="dsq_sb")
+                    add_first_two(dsq_sb, d_d[c + 1])
+                    add_third(dsq_sb, d_d[c + 1])
+                    dsq[c + 1] = dsq_sb[:]
+                invert_dsq(c + 1)
 
         final = N_PAIRS - 1
-        part_along_d(final)
-        cd_both = held.tile([C, T, S], F32, name="cd_both")
-        nc.vector.tensor_tensor(cd_both[:], cd[final][:, :, 0:S], cd[final][:, :, S:PAIR], ALU.add)
         out_ots = out.rearrange("(t o) s -> o t s", t=T)
-        result01 = held.tile([C, 2, S], F32, name="result01")
-        nc.vector.scalar_tensor_tensor(
-            result01[:], cd_both[:, 0:2, :], -REMOVED / K, a_mean01[:], ALU.mult, ALU.add
-        )
-        nc.sync.dma_start(out_ots[:, 0:2, :], result01[:])
-        result2 = held.tile([C, S], F32, name="result2")
-        nc.vector.scalar_tensor_tensor(
-            result2[:], cd_both[:, 2, :], -REMOVED / K, a_mean2[:], ALU.mult, ALU.add
-        )
-        nc.scalar.dma_start(out_ots[:, 2, :], result2[:])
+        cd_last = [held.tile([C, PAIR], F32, name=f"cd_last{t}") for t in range(T)]
+        cd_both = [held.tile([C, S], F32, name=f"cd_both{t}") for t in range(T)]
+        result = held.tile([C, T, S], F32, name="result")
+        a_mean = [a_mean01[:, 0, :], a_mean01[:, 1, :], a_mean2[:]]
+
+        def last_part_along_d(t):
+            nc.vector.tensor_tensor(cd_last[t][:], d_sb[final][:, t, :], coef[final][:], ALU.mult)
+
+        def both_neighbours(t):
+            nc.vector.tensor_tensor(cd_both[t][:], cd_last[t][:, 0:S], cd_last[t][:, S:PAIR], ALU.add)
+
+        def finish(t):
+            nc.vector.scalar_tensor_tensor(
+                result[:, t, :], cd_both[t][:], -REMOVED / K, a_mean[t], ALU.mult, ALU.add
+            )
+
+        last_part_along_d(0)
+        last_part_along_d(1)
+        both_neighbours(0)
+        last_part_along_d(2)
+        both_neighbours(1)
+        finish(0)
+        both_neighbours(2)
+        finish(1)
+        nc.sync.dma_start(out_ots[:, 0:2, :], result[:, 0:2, :])
+        finish(2)
+        nc.scalar.dma_start(out_ots[:, 2, :], result[:, 2, :])

@@ -14,7 +14,7 @@ K = 8
 N = K * S
 PAIR = 2 * S
 N_PAIRS = K // 2
-TENSOR_SUMS = 1
+TENSOR_SUMS = 2
 EPS = 1e-6
 REMOVED = 0.8
 
@@ -113,14 +113,17 @@ def tile_vn_pctransformer_kernel(tc, x, b1, w1, u1, offs, out):
             for t in range(T):
                 nc.scalar.copy(e_bf[c][:, t, :], e_f32[c][:, t, :])
 
-        def project(c):
+        def project_d(c):
+            for t in range(T):
+                d_ps[t] = psum_d.tile([C, PAIR], F32, name="d_ps")
+                nc.tensor.matmul(d_ps[t][:], u_sb[:, 0, :], e_bf[c][:, t, :], start=True, stop=False)
+                nc.tensor.matmul(d_ps[t][:], u_sb[:, 1, :], ctr_bf[:, t, :], start=False, stop=True)
+
+        def project_p(c):
             for t in range(T):
                 p_ps[t] = psum_p.tile([C, PAIR], F32, name="p_ps")
                 nc.tensor.matmul(p_ps[t][:], w_sb[:, 0, :], e_bf[c][:, t, :], start=True, stop=False)
                 nc.tensor.matmul(p_ps[t][:], w_sb[:, 1, :], ctr_bf[:, t, :], start=False, stop=True)
-                d_ps[t] = psum_d.tile([C, PAIR], F32, name="d_ps")
-                nc.tensor.matmul(d_ps[t][:], u_sb[:, 0, :], e_bf[c][:, t, :], start=True, stop=False)
-                nc.tensor.matmul(d_ps[t][:], u_sb[:, 1, :], ctr_bf[:, t, :], start=False, stop=True)
             for h in range(2):
                 cols = slice(h * S, (h + 1) * S)
                 nc.tensor.matmul(a_mean01[:], w_edge_mean[:], e_bf[c][:, 0:2, cols], start=False, stop=False)
@@ -177,18 +180,19 @@ def tile_vn_pctransformer_kernel(tc, x, b1, w1, u1, offs, out):
                     a_mean2[:], minus_removed[:], cd[c][:, 2, cols], start=False, stop=stop and h == 1
                 )
 
-        def project_and_square(c):
-            project(c)
+        def d_and_square(c):
+            project_d(c)
             copy_and_square_d(c)
-            if c < TENSOR_SUMS:
-                dsq_on_tensor(c)
 
         gather(0)
         round_edges(0)
-        project_and_square(0)
+        d_and_square(0)
+        project_p(0)
+        dsq_on_tensor(0)
         invert_dsq(0)
         gather(1)
         round_edges(1)
+        d_and_square(1)
         for c in range(N_PAIRS):
             if c + 2 < N_PAIRS:
                 gather(c + 2)
@@ -202,20 +206,26 @@ def tile_vn_pctransformer_kernel(tc, x, b1, w1, u1, offs, out):
             if c >= 1:
                 part_along_d(c - 1, 1)
                 part_along_d(c - 1, 2)
-            coefficient(c)
             if c + 1 < N_PAIRS:
-                project_and_square(c + 1)
-            if c >= 1:
-                remove_on_tensor(c - 1, stop=c == N_PAIRS - 1)
-            if c + 1 < N_PAIRS:
-                if c + 1 >= TENSOR_SUMS:
+                project_p(c + 1)
+                if c + 1 < TENSOR_SUMS:
+                    dsq_on_tensor(c + 1)
+                    invert_dsq(c + 1)
+                    coefficient(c)
+                else:
                     dsq_sb = lagging.tile([C, PAIR], F32, name="dsq_sb")
                     add_first_two(dsq_sb, d_d[c + 1])
+                    coefficient(c)
                     add_third(dsq_sb, d_d[c + 1])
                     dsq[c + 1] = dsq_sb[:]
-                invert_dsq(c + 1)
+                    invert_dsq(c + 1)
+            if c + 2 < N_PAIRS:
+                d_and_square(c + 2)
+            if c >= 1:
+                remove_on_tensor(c - 1, stop=c == N_PAIRS - 1)
 
         final = N_PAIRS - 1
+        coefficient(final)
         out_ots = out.rearrange("(t o) s -> o t s", t=T)
         cd_last = [held.tile([C, PAIR], F32, name=f"cd_last{t}") for t in range(T)]
         cd_both = [held.tile([C, S], F32, name=f"cd_both{t}") for t in range(T)]

import concourse.mybir as mybir
from concourse.masks import make_identity

F32 = mybir.dt.float32
BF16 = mybir.dt.bfloat16
U16 = mybir.dt.uint16
ALU = mybir.AluOpType
ACT = mybir.ActivationFunctionType

C = 128
T = 3
S = 256
K = 8
N = K * S
PAIR = 2 * S
N_PAIRS = K // 2
TENSOR_SUMS = 2
EPS = 1e-6
REMOVED = 0.8

FLOPS = 2 * 2 * T * (2 * C) * C * N


def tile_vn_pctransformer_kernel(tc, x, b1, w1, u1, offs, out):
    nc = tc.nc
    with (
        tc.tile_pool(name="held", bufs=1) as held,
        tc.tile_pool(name="work", bufs=N_PAIRS) as work,
        tc.tile_pool(name="lagging", bufs=N_PAIRS) as lagging,
        tc.psum_pool(name="psum_p", bufs=T) as psum_p,
        tc.psum_pool(name="psum_d", bufs=T) as psum_d,
        tc.psum_pool(name="psum_mean", bufs=1) as psum_mean,
    ):
        x_tcs = x.rearrange("(t c) s -> t c s", t=T)
        x_sb = held.tile([C, T, S], F32, name="x_sb")
        nc.sync.dma_start(x_sb[:, 0, :], x_tcs[0])
        nc.scalar.dma_start(x_sb[:, 1, :], x_tcs[1])
        nc.sync.dma_start(x_sb[:, 2, :], x_tcs[2])
        b1_sb = held.tile([C, 1], F32, name="b1_sb")
        nc.scalar.dma_start(b1_sb[:], b1)
        offsets = held.tile([C, N // 16], U16, name="offsets")
        nc.sync.dma_start(offsets[:], offs)
        w_sb = held.tile([C, 2, C], BF16, name="w_sb")
        nc.sync.dma_start(w_sb[:], w1.rearrange("(h i) o -> i h o", h=2))
        u_sb = held.tile([C, 2, C], BF16, name="u_sb")
        nc.sync.dma_start(u_sb[:], u1.rearrange("(h i) o -> i h o", h=2))

        eps_sb = held.tile([C, 1], F32, name="eps_sb")
        nc.gpsimd.memset(eps_sb[:], EPS)
        table_warmer = held.tile([C, 1], F32, name="table_warmer")
        nc.scalar.activation(table_warmer[:], eps_sb[:], ACT.Abs_reciprocal_sqrt)
        identity = held.tile([C, C], F32, name="identity")
        make_identity(nc, identity[:])
        minus_removed = held.tile([C, C], F32, name="minus_removed")
        nc.gpsimd.tensor_scalar_mul(minus_removed[:], identity[:], -REMOVED / K)
        w_edge_mean = held.tile([C, C], BF16, name="w_edge_mean")
        nc.gpsimd.tensor_scalar_mul(w_edge_mean[:], w_sb[:, 0, :], 1.0 / K)

        x_sq = held.tile([C, T, S], F32, name="x_sq")
        for t in range(T):
            nc.vector.tensor_tensor(x_sq[:, t, :], x_sb[:, t, :], x_sb[:, t, :], ALU.mult)
        x_len2 = held.tile([C, S], F32, name="x_len2")
        nc.vector.tensor_tensor(x_len2[:], x_sq[:, 0, :], x_sq[:, 1, :], ALU.add)
        nc.vector.tensor_tensor(x_len2[:], x_len2[:], x_sq[:, 2, :], ALU.add)
        x_rlen = held.tile([C, S], F32, name="x_rlen")
        nc.scalar.activation(x_rlen[:], x_len2[:], ACT.Abs_reciprocal_sqrt, bias=eps_sb[:])

        y = [held.tile([C, S], F32, name=f"y{t}") for t in range(T)]
        neg_y = held.tile([C, T, S], F32, name="neg_y")
        ctr_bf = held.tile([C, T, PAIR], BF16, name="ctr_bf")
        for t in range(T):
            nc.vector.scalar_tensor_tensor(
                y[t][:], x_sb[:, t, :], b1_sb[:, 0:1], x_rlen[:], ALU.mult, ALU.mult
            )
            nc.scalar.mul(neg_y[:, t, :], y[t][:], -1.0)
            nc.scalar.copy(
                ctr_bf[:, t, :].rearrange("c (h s) -> c h s", h=2),
                y[t][:].unsqueeze(1).to_broadcast([C, 2, S]),
            )

        a_mean01 = psum_mean.tile([C, 2, S], F32, name="a_mean01")
        a_mean2 = psum_mean.tile([C, S], F32, name="a_mean2")
        nc.tensor.matmul(a_mean01[:], w_sb[:, 1, :], ctr_bf[:, 0:2, 0:S], start=True, stop=False)
        nc.tensor.matmul(a_mean2[:], w_sb[:, 1, :], ctr_bf[:, 2, 0:S], start=True, stop=False)

        e_f32 = {}
        e_bf = {}
        p_ps = {}
        d_ps = {}
        d_sb = {}
        p_d = {}
        d_d = {}
        dot = {}
        coef = {}
        dsq = {}
        r_dsq = {}
        cd = {}

        def gather(c):
            e_f32[c] = work.tile([C, T, PAIR], F32, name="e_f32")
            for t in range(T):
                for h in range(2):
                    k = 2 * c + h
                    nc.vector.tensor_tensor(
                        e_f32[c][:, t, h * S : (h + 1) * S],
                        y[t][:].indirect(offsets[:, k * (S // 16) : (k + 1) * (S // 16)]),
                        neg_y[:, t, :],
                        ALU.add,
                    )

        def round_edges(c):
            e_bf[c] = work.tile([C, T, PAIR], BF16, name="e_bf")
            for t in range(T):
                nc.scalar.copy(e_bf[c][:, t, :], e_f32[c][:, t, :])

        def project_d(c):
            for t in range(T):
                d_ps[t] = psum_d.tile([C, PAIR], F32, name="d_ps")
                nc.tensor.matmul(d_ps[t][:], u_sb[:, 0, :], e_bf[c][:, t, :], start=True, stop=False)
                nc.tensor.matmul(d_ps[t][:], u_sb[:, 1, :], ctr_bf[:, t, :], start=False, stop=True)

        def project_p(c):
            for t in range(T):
                p_ps[t] = psum_p.tile([C, PAIR], F32, name="p_ps")
                nc.tensor.matmul(p_ps[t][:], w_sb[:, 0, :], e_bf[c][:, t, :], start=True, stop=False)
                nc.tensor.matmul(p_ps[t][:], w_sb[:, 1, :], ctr_bf[:, t, :], start=False, stop=True)
            for h in range(2):
                cols = slice(h * S, (h + 1) * S)
                nc.tensor.matmul(a_mean01[:], w_edge_mean[:], e_bf[c][:, 0:2, cols], start=False, stop=False)
                nc.tensor.matmul(a_mean2[:], w_edge_mean[:], e_bf[c][:, 2, cols], start=False, stop=False)

        def copy_and_square_d(c):
            d_sb[c] = lagging.tile([C, T, PAIR], F32, name="d_sb")
            d_d[c] = work.tile([C, T, PAIR], F32, name="d_d")
            for t in range(T):
                nc.scalar.copy(d_sb[c][:, t, :], d_ps[t][:])
                nc.scalar.activation(d_d[c][:, t, :], d_ps[t][:], ACT.Square)

        def dsq_on_tensor(c):
            dsq_ps = psum_d.tile([C, PAIR], F32, name="dsq_ps", tag="d_ps")
            dsq[c] = dsq_ps[:]
            for t in range(T):
                nc.tensor.matmul(dsq[c], identity[:], d_d[c][:, t, :], start=t == 0, stop=t == T - 1)

        def add_first_two(total, terms):
            nc.vector.tensor_tensor(total[:], terms[:, 0, :], terms[:, 1, :], ALU.add)

        def add_third(total, terms):
            nc.vector.tensor_tensor(total[:], total[:], terms[:, 2, :], ALU.add)

        def products(c):
            p_d[c] = work.tile([C, T, PAIR], F32, name="p_d")
            for t in range(T):
                nc.vector.tensor_tensor(p_d[c][:, t, :], p_ps[t][:], d_sb[c][:, t, :], ALU.mult)

        def invert_dsq(c):
            r_len = work.tile([C, PAIR], F32, name="r_len")
            nc.scalar.activation(r_len[:], dsq[c], ACT.Abs_reciprocal_sqrt, bias=eps_sb[:])
            r_dsq[c] = lagging.tile([C, PAIR], F32, name="r_dsq")
            nc.scalar.activation(r_dsq[c][:], r_len[:], ACT.Square)

        def coefficient(c):
            coef[c] = work.tile([C, PAIR], F32, name="coef")
            nc.vector.scalar_tensor_tensor(coef[c][:], dot[c][:], 0.0, r_dsq[c][:], ALU.min, ALU.mult)

        def part_along_d(c, t):
            if t == 0:
                cd[c] = work.tile([C, T, PAIR], F32, name="cd")
            nc.vector.tensor_tensor(cd[c][:, t, :], d_sb[c][:, t, :], coef[c][:], ALU.mult)

        def remove_on_tensor(c, stop):
            for h in range(2):
                cols = slice(h * S, (h + 1) * S)
                nc.tensor.matmul(
                    a_mean01[:], minus_removed[:], cd[c][:, 0:2, cols], start=False, stop=stop and h == 1
                )
            for h in range(2):
                cols = slice(h * S, (h + 1) * S)
                nc.tensor.matmul(
                    a_mean2[:], minus_removed[:], cd[c][:, 2, cols], start=False, stop=stop and h == 1
                )

        def d_and_square(c):
            project_d(c)
            copy_and_square_d(c)

        gather(0)
        round_edges(0)
        d_and_square(0)
        project_p(0)
        dsq_on_tensor(0)
        invert_dsq(0)
        gather(1)
        round_edges(1)
        d_and_square(1)
        for c in range(N_PAIRS):
            if c + 2 < N_PAIRS:
                gather(c + 2)
                round_edges(c + 2)
            products(c)
            dot[c] = lagging.tile([C, PAIR], F32, name="dot")
            add_first_two(dot[c], p_d[c])
            if c >= 1:
                part_along_d(c - 1, 0)
            add_third(dot[c], p_d[c])
            if c >= 1:
                part_along_d(c - 1, 1)
                part_along_d(c - 1, 2)
            if c + 1 < N_PAIRS:
                project_p(c + 1)
                if c + 1 < TENSOR_SUMS:
                    dsq_on_tensor(c + 1)
                    invert_dsq(c + 1)
                    coefficient(c)
                else:
                    dsq_sb = lagging.tile([C, PAIR], F32, name="dsq_sb")
                    add_first_two(dsq_sb, d_d[c + 1])
                    coefficient(c)
                    add_third(dsq_sb, d_d[c + 1])
                    dsq[c + 1] = dsq_sb[:]
                    invert_dsq(c + 1)
            if c + 2 < N_PAIRS:
                d_and_square(c + 2)
            if c >= 1:
                remove_on_tensor(c - 1, stop=c == N_PAIRS - 1)

        final = N_PAIRS - 1
        coefficient(final)
        out_ots = out.rearrange("(t o) s -> o t s", t=T)
        cd_last = [held.tile([C, PAIR], F32, name=f"cd_last{t}") for t in range(T)]
        cd_both = [held.tile([C, S], F32, name=f"cd_both{t}") for t in range(T)]
        result = held.tile([C, T, S], F32, name="result")
        a_mean = [a_mean01[:, 0, :], a_mean01[:, 1, :], a_mean2[:]]

        def last_part_along_d(t):
            nc.vector.tensor_tensor(cd_last[t][:], d_sb[final][:, t, :], coef[final][:], ALU.mult)

        def both_neighbours(t):
            nc.vector.tensor_tensor(cd_both[t][:], cd_last[t][:, 0:S], cd_last[t][:, S:PAIR], ALU.add)

        def finish(t):
            nc.vector.scalar_tensor_tensor(
                result[:, t, :], cd_both[t][:], -REMOVED / K, a_mean[t], ALU.mult, ALU.add
            )

        last_part_along_d(0)
        last_part_along_d(1)
        both_neighbours(0)
        last_part_along_d(2)
        both_neighbours(1)
        finish(0)
        both_neighbours(2)
        finish(1)
        nc.sync.dma_start(out_ots[:, 0:2, :], result[:, 0:2, :])
        finish(2)
        nc.scalar.dma_start(out_ots[:, 2, :], result[:, 2, :])
